import numpy as np
import ml_dtypes


def mxq(x, axis, fmt="e4m3"):
    dtype, down = {"e4m3": (ml_dtypes.float8_e4m3fn, 7), "e5m2": (ml_dtypes.float8_e5m2, 14)}[fmt]
    v = np.moveaxis(np.asarray(x, np.float32).astype(ml_dtypes.bfloat16).astype(np.float64), axis, -1)
    blocks = v.reshape(v.shape[:-1] + (-1, 32))
    amax = np.abs(blocks).max(-1, keepdims=True)
    byte = np.maximum(np.where(amax > 0, np.frexp(amax)[1] - 1 + 127, 0) - down, 1)
    scale = np.exp2(byte - 127.0)
    codes = (blocks / scale).astype(np.float32).astype(dtype).astype(np.float64)
    return np.moveaxis((codes * scale).reshape(v.shape), -1, axis)


WIDE = False


def mx_kscale(k):
    if not WIDE:
        return np.ones(k)
    levels = np.array([30, -30])
    if k % 512:
        return np.exp2(np.random.permutation(np.resize(levels, k // 32))).repeat(32)
    a = np.empty((k // 512, 16))
    for p in range(k // 512):
        a[p, :8] = np.random.permutation(np.resize(levels, 8))
        for g in range(8):
            far = levels[np.abs(levels - a[p, g]) >= 10]
            a[p, g + 8] = far[np.random.randint(len(far))]
    return np.exp2(a.ravel()).repeat(32)


BF16 = ml_dtypes.bfloat16


def bf(x):
    return np.asarray(x, np.float32).astype(BF16)


def f64(x):
    return np.asarray(x).astype(np.float64)


N, C, E, T, H, CK = 3, 512, 512, 1024, 8, 64
EPS = 1e-5


def setup_inputs():
    s = mx_kscale(C)
    return {
        "h_attn": bf(np.random.standard_normal((N, T, C)) * 0.4 * s),
        "x": bf(np.random.standard_normal((N, E, T))),
        "masks": bf(np.random.uniform(0.2, 1.0, (N, 1, T))),
        "Wo": bf(np.random.standard_normal((E, C)) * 2.0 / np.sqrt(C) / s[None, :]),
        "bo": bf(np.random.standard_normal(E) * 0.5),
    }


def reference(h_attn, x, masks, Wo, bo):
    o = (mxq(f64(h_attn), 2, "e5m2") @ mxq(f64(Wo), 1, "e4m3").T) + f64(bo)
    y = o.transpose(0, 2, 1) * f64(masks) + f64(x)
    mean = y.mean(-1, keepdims=True)
    var = np.square(y - mean).mean(-1, keepdims=True)
    return (y - mean) / np.sqrt(var + EPS)

@@ -1,0 +1,271 @@
+from contextlib import ExitStack
+
+import concourse.mybir as mybir
+from concourse.masks import make_identity
+
+N, T, C, E = 3, 1024, 512, 512
+EPS = 1e-5
+FLOPS = 2 * N * T * C * E
+
+F32 = mybir.dt.float32
+BF16 = mybir.dt.bfloat16
+U32 = mybir.dt.uint32
+U8 = mybir.dt.uint8
+E4M3 = mybir.dt.float8_e4m3fn_x4
+E5M2 = mybir.dt.float8_e5m2_x4
+ALU = mybir.AluOpType
+ACT = mybir.ActivationFunctionType
+
+P = 128
+HALF = 512
+GROUP = 256
+SLOTS = E // P
+TILES = N * SLOTS
+GROUPS = N * T // GROUP
+POOL_COLS = 768
+
+
+def tile_transformerencoderblock_pa_kernel(tc, h_attn, x, masks, Wo, bo, out):
+    nc = tc.nc
+    with ExitStack() as ctx:
+        keep = ctx.enter_context(tc.tile_pool(name="keep", bufs=1))
+        work = ctx.enter_context(tc.tile_pool(name="work", bufs=3))
+        stat = ctx.enter_context(tc.tile_pool(name="stat", bufs=TILES))
+        psum = ctx.enter_context(tc.psum_pool(name="psum", bufs=1))
+        ctx.enter_context(tc.manual_schedule())
+
+        h_rows = h_attn.rearrange("n (g p j) k -> (n g) p j k", p=P, j=2)
+        w_rows = Wo.rearrange("(p j) k -> p j k", j=SLOTS)
+        x_rows = x.rearrange("n (p j) t -> n j p t", j=SLOTS)
+        out_rows = out.rearrange("n (p j) t -> n j p t", j=SLOTS)
+        mask_halves = masks.rearrange("n o (h t) -> (n o h) t", t=HALF)
+
+        ident = keep.tile([P, P], F32, name="ident")
+        make_identity(nc, ident[:])
+        minus_half = keep.tile([P, 1], F32, name="minus_half")
+        nc.gpsimd.memset(minus_half[:], -0.5)
+        mask_rows = keep.tile([P, HALF], BF16, name="mask_rows")
+        nc.vector.memset(mask_rows[:], 0.0)
+        nc.scalar.dma_start(out=mask_rows[0:2, :], in_=mask_halves[0:2, :])
+        bias = keep.tile([P, SLOTS], BF16, name="bias")
+        nc.scalar.dma_start(out=bias[:], in_=bo.rearrange("(p j) -> p j", j=SLOTS))
+        nc.scalar.dma_start(out=mask_rows[2:6, :], in_=mask_halves[2:6, :])
+        pick = keep.tile([P, 8], BF16, name="pick")
+        nc.scalar.activation(out=pick[:], in_=ident[:, 0:8], func=ACT.Identity)
+
+        h_raw, w_raw, x_sb = {}, {}, {}
+
+        def load_h(g):
+            h_raw[g] = keep.tile([P, 2, C], BF16, name="h_raw%d" % g)
+            nc.sync.dma_start(out=h_raw[g][:], in_=h_rows[g])
+
+        def load_w(pair):
+            w_raw[pair] = keep.tile([P, 2, C], BF16, name="w_raw%d" % pair)
+            nc.sync.dma_start(out=w_raw[pair][:], in_=w_rows[:, 2 * pair : 2 * pair + 2, :])
+
+        def load_x(i):
+            x_sb[i] = keep.tile([P, T], BF16, name="x_sb%d" % i)
+            nc.sync.dma_start(out=x_sb[i][:], in_=x_rows[i // SLOTS, i % SLOTS])
+
+        load_h(0)
+        load_w(0)
+        load_h(1)
+        load_h(2)
+        load_h(3)
+        load_w(1)
+        for i in range(TILES):
+            if i + 4 < GROUPS:
+                load_h(i + 4)
+            load_x(i)
+
+        w_codes = keep.tile([P, E], U32, name="w_codes", align_bytes=64)
+        w_scales = keep.tile([P, E], U8, name="w_scales", align_bytes=64)
+        h_codes, h_scales = {}, {}
+        for c in range(N * T // HALF):
+            h_codes[c] = keep.tile([P, HALF], U32, name="h_codes%d" % c, align_bytes=64)
+            h_scales[c] = keep.tile([P, HALF], U8, name="h_scales%d" % c, align_bytes=64)
+
+        banks, grouped = {}, {}
+
+        def transpose(key, raw):
+            words = raw[:].rearrange("p j k -> p (j k)").bitcast(F32)
+            banks[key] = psum.tile([P, 2, 2, P], F32, name="turned", bufs=3)
+            for j in range(2):
+                for u in range(2):
+                    nc.tensor.transpose(
+                        banks[key][:, j, u, :], words[:, 256 * j + u : 256 * (j + 1) : 2], ident[:]
+                    )
+
+        def gather(key, copy, order):
+            grouped[key] = work.tile([P, 4 * GROUP], BF16, name="grouped", align_bytes=64)
+            dst = grouped[key][:].bitcast(F32)
+            if order == "h":
+                copy(out=dst.rearrange("p (r j u) -> p r j u", j=2, u=2),
+                     in_=banks[key][:].rearrange("p j u r -> p r j u"))
+            else:
+                copy(out=dst.rearrange("p (j r u) -> p j r u", j=2, u=2),
+                     in_=banks[key][:].rearrange("p j u r -> p j r u"))
+
+        def quantize_h(g):
+            cols = slice(GROUP * (g % 2), GROUP * (g % 2 + 1))
+            nc.vector.quantize_mx(
+                out=h_codes[g // 2][:, cols].bitcast(E5M2), scales=h_scales[g // 2][:, cols], in_=grouped[g][:]
+            )
+
+        def quantize_w(pair):
+            cols = slice(2 * P * pair, 2 * P * (pair + 1))
+            nc.vector.quantize_mx(
+                out=w_codes[:, cols].bitcast(E4M3), scales=w_scales[:, cols], in_=grouped[("w", pair)][:]
+            )
+
+        mask_bank, mask_all = {}, {}
+
+        def spread_mask(n):
+            mask_bank[n] = psum.tile([P, T], BF16, name="mask_bank", bufs=1)
+            for h in range(2):
+                r = 2 * n + h
+                nc.tensor.matmul(
+                    mask_bank[n][:, HALF * h : HALF * (h + 1)],
+                    lhsT=pick[:, r : r + 1].to_broadcast([P, P]),
+                    rhs=mask_rows[:],
+                    start=True,
+                    stop=True,
+                )
+
+        def copy_mask(n):
+            mask_all[n] = keep.tile([P, T], BF16, name="mask_all%d" % n)
+            nc.scalar.copy(out=mask_all[n][:], in_=mask_bank[n][:])
+
+        acc, masked, y, res = {}, {}, {}, {}
+        total, neg_mean, squares, var, rstd, shift = {}, {}, {}, {}, {}, {}
+
+        def project(i, h):
+            n, j = divmod(i, SLOTS)
+            cols = slice(P * j, P * (j + 1))
+            acc[i, h] = psum.tile([P, HALF], F32, name="acc", bufs=4)
+            nc.tensor.matmul_mx(
+                out=acc[i, h][:],
+                lhsT=w_codes[:, cols].bitcast(E4M3),
+                lhsT_scale=w_scales[:, cols],
+                rhs=h_codes[2 * n + h][:].bitcast(E5M2),
+                rhs_scale=h_scales[2 * n + h][:],
+                start=True,
+                stop=True,
+            )
+
+        def bias_and_mask(i, h):
+            n, j = divmod(i, SLOTS)
+            if h == 0:
+                masked[i] = work.tile([P, T], F32, name="masked")
+            cols = slice(HALF * h, HALF * (h + 1))
+            nc.vector.scalar_tensor_tensor(
+                out=masked[i][:, cols], in0=acc[i, h][:], scalar=bias[:, j : j + 1],
+                in1=mask_all[n][:, cols], op0=ALU.add, op1=ALU.mult,
+            )
+
+        def add_residual(i):
+            y[i] = work.tile([P, T], F32, name="y", bufs=4)
+            total[i] = stat.tile([P, 1], F32, name="total")
+            nc.vector.scalar_tensor_tensor(
+                out=y[i][:], in0=masked[i][:], scalar=1.0, in1=x_sb[i][:],
+                op0=ALU.mult, op1=ALU.add, accum_out=total[i][:],
+            )
+            neg_mean[i] = stat.tile([P, 1], F32, name="neg_mean")
+            nc.gpsimd.tensor_scalar(
+                out=neg_mean[i][:], in0=total[i][:], scalar1=-1.0 / T, scalar2=0.0, op0=ALU.mult, op1=ALU.add
+            )
+
+        def sum_squares(i):
+            squared = work.tile([P, T], BF16, name="squared", bufs=2)
+            squares[i] = stat.tile([P, 1], F32, name="squares")
+            nc.scalar.activation(
+                out=squared[:], in_=y[i][:], func=ACT.Square, scale=-float(T), bias=total[i][:],
+                accum_out=squares[i][:],
+            )
+            var[i] = stat.tile([P, 1], F32, name="var")
+            nc.scalar.activation(
+                out=var[i][:], in_=squares[i][:], func=ACT.Identity, scale=1.0 / T**3, bias=EPS
+            )
+            rstd[i] = stat.tile([P, 1], F32, name="rstd")
+            nc.gpsimd.tensor_tensor(out=rstd[i][:], in0=var[i][:], in1=minus_half[:], op=ALU.pow)
+
+        def normalise_scalar(i):
+            res[i] = work.tile([P, T], F32, name="res", bufs=TILES)
+            shift[i] = stat.tile([P, 1], F32, name="shift")
+            nc.scalar.activation(out=shift[i][:], in_=neg_mean[i][:], func=ACT.Identity, scale=rstd[i][:])
+            nc.scalar.activation(
+                out=res[i][:, POOL_COLS:], in_=y[i][:, POOL_COLS:], func=ACT.Identity,
+                scale=rstd[i][:], bias=shift[i][:],
+            )
+
+        def normalise_pool(i):
+            nc.gpsimd.tensor_scalar(
+                out=res[i][:, :POOL_COLS], in0=y[i][:, :POOL_COLS], scalar1=neg_mean[i][:], scalar2=rstd[i][:],
+                op0=ALU.add, op1=ALU.mult,
+            )
+            nc.sync.dma_start(out=out_rows[i // SLOTS, i % SLOTS], in_=res[i][:])
+
+        def normalise_vector(i):
+            res[i] = work.tile([P, T], F32, name="res", bufs=TILES)
+            for h in range(2):
+                cols = slice(HALF * h, HALF * (h + 1))
+                nc.vector.tensor_scalar(
+                    out=res[i][:, cols], in0=y[i][:, cols], scalar1=neg_mean[i][:], scalar2=rstd[i][:],
+                    op0=ALU.add, op1=ALU.mult,
+                )
+                nc.sync.dma_start(out=out_rows[i // SLOTS, i % SLOTS][:, cols], in_=res[i][:, cols])
+
+        spread_mask(0)
+        copy_mask(0)
+        transpose(0, h_raw[0])
+        gather(0, nc.vector.tensor_copy, "h")
+        transpose(("w", 0), w_raw[0])
+        gather(("w", 0), nc.scalar.copy, "w")
+        transpose(1, h_raw[1])
+        gather(1, nc.vector.tensor_copy, "h")
+        quantize_h(0)
+        quantize_w(0)
+        quantize_h(1)
+        transpose(2, h_raw[2])
+        gather(2, nc.scalar.copy, "h")
+        project(0, 0)
+        transpose(3, h_raw[3])
+        gather(3, nc.scalar.copy, "h")
+        quantize_h(2)
+        bias_and_mask(0, 0)
+        quantize_h(3)
+        project(0, 1)
+        project(1, 0)
+        transpose(("w", 1), w_raw[1])
+        gather(("w", 1), nc.scalar.copy, "w")
+        bias_and_mask(0, 1)
+        transpose(4, h_raw[4])
+        gather(4, nc.scalar.copy, "h")
+        quantize_w(1)
+
+        for i in range(1, TILES + 1):
+            if i + 4 < GROUPS:
+                transpose(i + 4, h_raw[i + 4])
+            if i < TILES:
+                bias_and_mask(i, 0)
+            if i + 3 < GROUPS:
+                quantize_h(i + 3)
+            if i < TILES:
+                project(i, 1)
+            if i + 4 < GROUPS:
+                gather(i + 4, nc.scalar.copy, "h")
+            if i % SLOTS == 2 and i // SLOTS + 1 < N:
+                spread_mask(i // SLOTS + 1)
+                copy_mask(i // SLOTS + 1)
+            if 2 <= i < TILES:
+                normalise_scalar(i - 2)
+            add_residual(i - 1)
+            if 2 <= i < TILES:
+                normalise_pool(i - 2)
+            sum_squares(i - 1)
+            if i < TILES:
+                bias_and_mask(i, 1)
+            if i + 1 < TILES:
+                project(i + 1, 0)
+        normalise_vector(TILES - 2)
+        normalise_vector(TILES - 1)

@@ -22,7 +22,7 @@ GROUP = 256
 SLOTS = E // P
 TILES = N * SLOTS
 GROUPS = N * T // GROUP
-POOL_COLS = 768
+ON_VECTOR = (4, 9, 10, 11)
 
 
 def tile_transformerencoderblock_pa_kernel(tc, h_attn, x, masks, Wo, bo, out):
@@ -38,20 +38,19 @@ def tile_transformerencoderblock_pa_kernel(tc, h_attn, x, masks, Wo, bo, out):
         w_rows = Wo.rearrange("(p j) k -> p j k", j=SLOTS)
         x_rows = x.rearrange("n (p j) t -> n j p t", j=SLOTS)
         out_rows = out.rearrange("n (p j) t -> n j p t", j=SLOTS)
-        mask_halves = masks.rearrange("n o (h t) -> (n o h) t", t=HALF)
+        mask_halves = masks.rearrange("n o (h t) -> (o h) n t", t=HALF)
 
+        first_rows = keep.tile([P, HALF], BF16, name="first_rows")
+        nc.gpsimd.memset(first_rows[:].bitcast(U32), 0)
+        nc.scalar.dma_start(out=first_rows[0:2, :], in_=mask_halves[:, 0, :])
         ident = keep.tile([P, P], F32, name="ident")
         make_identity(nc, ident[:])
+        later_rows = keep.tile([P, N - 1, HALF], BF16, name="later_rows")
+        nc.vector.memset(later_rows[:], 0.0)
+        pick = keep.tile([P, 2], BF16, name="pick")
+        nc.scalar.activation(out=pick[:], in_=ident[:, 0:2], func=ACT.Identity)
         minus_half = keep.tile([P, 1], F32, name="minus_half")
         nc.gpsimd.memset(minus_half[:], -0.5)
-        mask_rows = keep.tile([P, HALF], BF16, name="mask_rows")
-        nc.vector.memset(mask_rows[:], 0.0)
-        nc.scalar.dma_start(out=mask_rows[0:2, :], in_=mask_halves[0:2, :])
-        bias = keep.tile([P, SLOTS], BF16, name="bias")
-        nc.scalar.dma_start(out=bias[:], in_=bo.rearrange("(p j) -> p j", j=SLOTS))
-        nc.scalar.dma_start(out=mask_rows[2:6, :], in_=mask_halves[2:6, :])
-        pick = keep.tile([P, 8], BF16, name="pick")
-        nc.scalar.activation(out=pick[:], in_=ident[:, 0:8], func=ACT.Identity)
 
         h_raw, w_raw, x_sb = {}, {}, {}
 
@@ -72,10 +71,14 @@ def tile_transformerencoderblock_pa_kernel(tc, h_attn, x, masks, Wo, bo, out):
         load_h(1)
         load_h(2)
         load_h(3)
+        bias = keep.tile([P, SLOTS], BF16, name="bias")
+        nc.sync.dma_start(out=bias[:], in_=bo.rearrange("(p j) -> p j", j=SLOTS))
+        load_x(0)
         load_w(1)
-        for i in range(TILES):
-            if i + 4 < GROUPS:
-                load_h(i + 4)
+        nc.sync.dma_start(out=later_rows[0:2], in_=mask_halves[:, 1:, :])
+        for i in range(1, TILES):
+            if i + 3 < GROUPS:
+                load_h(i + 3)
             load_x(i)
 
         w_codes = keep.tile([P, E], U32, name="w_codes", align_bytes=64)
@@ -89,7 +92,7 @@ def tile_transformerencoderblock_pa_kernel(tc, h_attn, x, masks, Wo, bo, out):
 
         def transpose(key, raw):
             words = raw[:].rearrange("p j k -> p (j k)").bitcast(F32)
-            banks[key] = psum.tile([P, 2, 2, P], F32, name="turned", bufs=3)
+            banks[key] = psum.tile([P, 2, 2, P], F32, name="turned", tag="turned", bufs=4)
             for j in range(2):
                 for u in range(2):
                     nc.tensor.transpose(
@@ -121,23 +124,28 @@ def tile_transformerencoderblock_pa_kernel(tc, h_attn, x, masks, Wo, bo, out):
         mask_bank, mask_all = {}, {}
 
         def spread_mask(n):
-            mask_bank[n] = psum.tile([P, T], BF16, name="mask_bank", bufs=1)
+            mask_bank[n] = psum.tile([P, T], BF16, name="mask_bank", tag="turned", bufs=4)
             for h in range(2):
-                r = 2 * n + h
                 nc.tensor.matmul(
                     mask_bank[n][:, HALF * h : HALF * (h + 1)],
-                    lhsT=pick[:, r : r + 1].to_broadcast([P, P]),
-                    rhs=mask_rows[:],
+                    lhsT=pick[:, h : h + 1].to_broadcast([P, P]),
+                    rhs=first_rows[:] if n == 0 else later_rows[:, n - 1, :],
                     start=True,
                     stop=True,
                 )
-
-        def copy_mask(n):
             mask_all[n] = keep.tile([P, T], BF16, name="mask_all%d" % n)
             nc.scalar.copy(out=mask_all[n][:], in_=mask_bank[n][:])
 
+        def turn_h(g, copy):
+            transpose(g, h_raw[g])
+            gather(g, copy, "h")
+
+        def turn_w(pair, copy):
+            transpose(("w", pair), w_raw[pair])
+            gather(("w", pair), copy, "w")
+
         acc, masked, y, res = {}, {}, {}, {}
-        total, neg_mean, squares, var, rstd, shift = {}, {}, {}, {}, {}, {}
+        total, neg_mean, squares, rstd, shift = {}, {}, {}, {}, {}
 
         def project(i, h):
             n, j = divmod(i, SLOTS)
@@ -164,16 +172,17 @@ def tile_transformerencoderblock_pa_kernel(tc, h_attn, x, masks, Wo, bo, out):
             )
 
         def add_residual(i):
-            y[i] = work.tile([P, T], F32, name="y", bufs=4)
+            y[i] = work.tile([P, T], F32, name="y", bufs=5)
             total[i] = stat.tile([P, 1], F32, name="total")
             nc.vector.scalar_tensor_tensor(
                 out=y[i][:], in0=masked[i][:], scalar=1.0, in1=x_sb[i][:],
                 op0=ALU.mult, op1=ALU.add, accum_out=total[i][:],
             )
-            neg_mean[i] = stat.tile([P, 1], F32, name="neg_mean")
-            nc.gpsimd.tensor_scalar(
-                out=neg_mean[i][:], in0=total[i][:], scalar1=-1.0 / T, scalar2=0.0, op0=ALU.mult, op1=ALU.add
-            )
+            if i in ON_VECTOR:
+                neg_mean[i] = stat.tile([P, 1], F32, name="neg_mean")
+                nc.gpsimd.tensor_scalar(
+                    out=neg_mean[i][:], in0=total[i][:], scalar1=-1.0 / T, scalar2=0.0, op0=ALU.mult, op1=ALU.add
+                )
 
         def sum_squares(i):
             squared = work.tile([P, T], BF16, name="squared", bufs=2)
@@ -182,33 +191,30 @@ def tile_transformerencoderblock_pa_kernel(tc, h_attn, x, masks, Wo, bo, out):
                 out=squared[:], in_=y[i][:], func=ACT.Square, scale=-float(T), bias=total[i][:],
                 accum_out=squares[i][:],
             )
-            var[i] = stat.tile([P, 1], F32, name="var")
-            nc.scalar.activation(
-                out=var[i][:], in_=squares[i][:], func=ACT.Identity, scale=1.0 / T**3, bias=EPS
-            )
+
+        def inverse_std(i):
+            var = stat.tile([P, 1], F32, name="var")
+            nc.scalar.activation(out=var[:], in_=squares[i][:], func=ACT.Identity, scale=1.0 / T**3, bias=EPS)
             rstd[i] = stat.tile([P, 1], F32, name="rstd")
-            nc.gpsimd.tensor_tensor(out=rstd[i][:], in0=var[i][:], in1=minus_half[:], op=ALU.pow)
+            nc.gpsimd.tensor_tensor(out=rstd[i][:], in0=var[:], in1=minus_half[:], op=ALU.pow)
+            if i not in ON_VECTOR:
+                shift[i] = stat.tile([P, 1], F32, name="shift")
+                nc.gpsimd.tensor_scalar(
+                    out=shift[i][:], in0=total[i][:], scalar1=rstd[i][:], scalar2=-1.0 / T,
+                    op0=ALU.mult, op1=ALU.mult,
+                )
 
         def normalise_scalar(i):
             res[i] = work.tile([P, T], F32, name="res", bufs=TILES)
-            shift[i] = stat.tile([P, 1], F32, name="shift")
-            nc.scalar.activation(out=shift[i][:], in_=neg_mean[i][:], func=ACT.Identity, scale=rstd[i][:])
             nc.scalar.activation(
-                out=res[i][:, POOL_COLS:], in_=y[i][:, POOL_COLS:], func=ACT.Identity,
-                scale=rstd[i][:], bias=shift[i][:],
-            )
-
-        def normalise_pool(i):
-            nc.gpsimd.tensor_scalar(
-                out=res[i][:, :POOL_COLS], in0=y[i][:, :POOL_COLS], scalar1=neg_mean[i][:], scalar2=rstd[i][:],
-                op0=ALU.add, op1=ALU.mult,
+                out=res[i][:], in_=y[i][:], func=ACT.Identity, scale=rstd[i][:], bias=shift[i][:],
             )
             nc.sync.dma_start(out=out_rows[i // SLOTS, i % SLOTS], in_=res[i][:])
 
-        def normalise_vector(i):
+        def normalise_vector(i, parts):
             res[i] = work.tile([P, T], F32, name="res", bufs=TILES)
-            for h in range(2):
-                cols = slice(HALF * h, HALF * (h + 1))
+            for h in range(parts):
+                cols = slice(T // parts * h, T // parts * (h + 1))
                 nc.vector.tensor_scalar(
                     out=res[i][:, cols], in0=y[i][:, cols], scalar1=neg_mean[i][:], scalar2=rstd[i][:],
                     op0=ALU.add, op1=ALU.mult,
@@ -216,36 +222,34 @@ def tile_transformerencoderblock_pa_kernel(tc, h_attn, x, masks, Wo, bo, out):
                 nc.sync.dma_start(out=out_rows[i // SLOTS, i % SLOTS][:, cols], in_=res[i][:, cols])
 
         spread_mask(0)
-        copy_mask(0)
-        transpose(0, h_raw[0])
-        gather(0, nc.vector.tensor_copy, "h")
-        transpose(("w", 0), w_raw[0])
-        gather(("w", 0), nc.scalar.copy, "w")
-        transpose(1, h_raw[1])
-        gather(1, nc.vector.tensor_copy, "h")
+        turn_h(0, nc.vector.tensor_copy)
+        turn_w(0, nc.scalar.copy)
+        turn_h(1, nc.vector.tensor_copy)
+        turn_h(2, nc.scalar.copy)
+        turn_h(3, nc.scalar.copy)
         quantize_h(0)
         quantize_w(0)
         quantize_h(1)
-        transpose(2, h_raw[2])
-        gather(2, nc.scalar.copy, "h")
         project(0, 0)
-        transpose(3, h_raw[3])
-        gather(3, nc.scalar.copy, "h")
+        project(1, 0)
         quantize_h(2)
-        bias_and_mask(0, 0)
         quantize_h(3)
         project(0, 1)
-        project(1, 0)
-        transpose(("w", 1), w_raw[1])
-        gather(("w", 1), nc.scalar.copy, "w")
+        project(1, 1)
+        turn_w(1, nc.scalar.copy)
+        bias_and_mask(0, 0)
+        bias_and_mask(1, 0)
         bias_and_mask(0, 1)
-        transpose(4, h_raw[4])
-        gather(4, nc.scalar.copy, "h")
         quantize_w(1)
+        turn_h(4, nc.scalar.copy)
+        project(2, 0)
+        add_residual(0)
+        turn_h(5, nc.scalar.copy)
+        sum_squares(0)
+        bias_and_mask(1, 1)
+        quantize_h(4)
 
-        for i in range(1, TILES + 1):
-            if i + 4 < GROUPS:
-                transpose(i + 4, h_raw[i + 4])
+        for i in range(2, TILES + 1):
             if i < TILES:
                 bias_and_mask(i, 0)
             if i + 3 < GROUPS:
@@ -253,19 +257,20 @@ def tile_transformerencoderblock_pa_kernel(tc, h_attn, x, masks, Wo, bo, out):
             if i < TILES:
                 project(i, 1)
             if i + 4 < GROUPS:
-                gather(i + 4, nc.scalar.copy, "h")
-            if i % SLOTS == 2 and i // SLOTS + 1 < N:
-                spread_mask(i // SLOTS + 1)
-                copy_mask(i // SLOTS + 1)
-            if 2 <= i < TILES:
-                normalise_scalar(i - 2)
+                turn_h(i + 4, nc.scalar.copy)
+            if i - 1 < N:
+                spread_mask(i - 1)
+            inverse_std(i - 2)
+            if i >= 3 and i - 3 not in ON_VECTOR:
+                normalise_scalar(i - 3)
             add_residual(i - 1)
-            if 2 <= i < TILES:
-                normalise_pool(i - 2)
             sum_squares(i - 1)
             if i < TILES:
                 bias_and_mask(i, 1)
+            if i - 3 in ON_VECTOR:
+                normalise_vector(i - 3, 1)
             if i + 1 < TILES:
                 project(i + 1, 0)
-        normalise_vector(TILES - 2)
-        normalise_vector(TILES - 1)
+        normalise_vector(TILES - 2, 1)
+        inverse_std(TILES - 1)
+        normalise_vector(TILES - 1, 2)

@@ -22,7 +22,12 @@ GROUP = 256
 SLOTS = E // P
 TILES = N * SLOTS
 GROUPS = N * T // GROUP
-ON_VECTOR = (4, 9, 10, 11)
+BLOCKS = T // P
+POOL_COLS = 640
+POOL_TILES = 8
+LAST = N - 1
+FIRST_LAST_TILE = TILES
+FIRST_LAST_GROUP = LAST * T // GROUP
 
 
 def tile_transformerencoderblock_pa_kernel(tc, h_attn, x, masks, Wo, bo, out):
@@ -31,26 +36,24 @@ def tile_transformerencoderblock_pa_kernel(tc, h_attn, x, masks, Wo, bo, out):
         keep = ctx.enter_context(tc.tile_pool(name="keep", bufs=1))
         work = ctx.enter_context(tc.tile_pool(name="work", bufs=3))
         stat = ctx.enter_context(tc.tile_pool(name="stat", bufs=TILES))
-        psum = ctx.enter_context(tc.psum_pool(name="psum", bufs=1))
+        psum = ctx.enter_context(tc.psum_pool(name="psum", bufs=8))
         ctx.enter_context(tc.manual_schedule())
 
         h_rows = h_attn.rearrange("n (g p j) k -> (n g) p j k", p=P, j=2)
         w_rows = Wo.rearrange("(p j) k -> p j k", j=SLOTS)
         x_rows = x.rearrange("n (p j) t -> n j p t", j=SLOTS)
         out_rows = out.rearrange("n (p j) t -> n j p t", j=SLOTS)
-        mask_halves = masks.rearrange("n o (h t) -> (o h) n t", t=HALF)
 
+        mask_halves = masks.rearrange("n o (h t) -> (o h) n t", t=HALF)
         first_rows = keep.tile([P, HALF], BF16, name="first_rows")
         nc.gpsimd.memset(first_rows[:].bitcast(U32), 0)
-        nc.scalar.dma_start(out=first_rows[0:2, :], in_=mask_halves[:, 0, :])
+        nc.sync.dma_start(out=first_rows[0:2, :], in_=mask_halves[:, 0, :])
         ident = keep.tile([P, P], F32, name="ident")
         make_identity(nc, ident[:])
         later_rows = keep.tile([P, N - 1, HALF], BF16, name="later_rows")
         nc.vector.memset(later_rows[:], 0.0)
         pick = keep.tile([P, 2], BF16, name="pick")
         nc.scalar.activation(out=pick[:], in_=ident[:, 0:2], func=ACT.Identity)
-        minus_half = keep.tile([P, 1], F32, name="minus_half")
-        nc.gpsimd.memset(minus_half[:], -0.5)
 
         h_raw, w_raw, x_sb = {}, {}, {}
 
@@ -75,11 +78,13 @@ def tile_transformerencoderblock_pa_kernel(tc, h_attn, x, masks, Wo, bo, out):
         nc.sync.dma_start(out=bias[:], in_=bo.rearrange("(p j) -> p j", j=SLOTS))
         load_x(0)
         load_w(1)
-        nc.sync.dma_start(out=later_rows[0:2], in_=mask_halves[:, 1:, :])
+        load_h(4)
         for i in range(1, TILES):
-            if i + 3 < GROUPS:
-                load_h(i + 3)
+            if i + 4 < GROUPS:
+                load_h(i + 4)
             load_x(i)
+            if i == 1:
+                nc.sync.dma_start(out=later_rows[0:2], in_=mask_halves[:, 1:, :])
 
         w_codes = keep.tile([P, E], U32, name="w_codes", align_bytes=64)
         w_scales = keep.tile([P, E], U8, name="w_scales", align_bytes=64)
@@ -88,26 +93,22 @@ def tile_transformerencoderblock_pa_kernel(tc, h_attn, x, masks, Wo, bo, out):
             h_codes[c] = keep.tile([P, HALF], U32, name="h_codes%d" % c, align_bytes=64)
             h_scales[c] = keep.tile([P, HALF], U8, name="h_scales%d" % c, align_bytes=64)
 
-        banks, grouped = {}, {}
+        grouped = {}
 
-        def transpose(key, raw):
+        def turn(key, raw, copy, src_order, dst_order):
             words = raw[:].rearrange("p j k -> p (j k)").bitcast(F32)
-            banks[key] = psum.tile([P, 2, 2, P], F32, name="turned", tag="turned", bufs=4)
+            bank = psum.tile([P, 2, 2, P], F32, name="turned", tag="bank")
             for j in range(2):
                 for u in range(2):
-                    nc.tensor.transpose(
-                        banks[key][:, j, u, :], words[:, 256 * j + u : 256 * (j + 1) : 2], ident[:]
-                    )
+                    nc.tensor.transpose(bank[:, j, u, :], words[:, 256 * j + u : 256 * (j + 1) : 2], ident[:])
+            grouped[key] = work.tile([P, 4 * GROUP], BF16, name="grouped", align_bytes=64, bufs=4)
+            copy(out=grouped[key][:].bitcast(F32).rearrange(dst_order, j=2, u=2), in_=bank[:].rearrange(src_order))
 
-        def gather(key, copy, order):
-            grouped[key] = work.tile([P, 4 * GROUP], BF16, name="grouped", align_bytes=64)
-            dst = grouped[key][:].bitcast(F32)
-            if order == "h":
-                copy(out=dst.rearrange("p (r j u) -> p r j u", j=2, u=2),
-                     in_=banks[key][:].rearrange("p j u r -> p r j u"))
-            else:
-                copy(out=dst.rearrange("p (j r u) -> p j r u", j=2, u=2),
-                     in_=banks[key][:].rearrange("p j u r -> p j r u"))
+        def turn_h(g, copy):
+            turn(g, h_raw[g], copy, "p j u r -> p r j u", "p (r j u) -> p r j u")
+
+        def turn_w(pair, copy):
+            turn(("w", pair), w_raw[pair], copy, "p j u r -> p j r u", "p (j r u) -> p j r u")
 
         def quantize_h(g):
             cols = slice(GROUP * (g % 2), GROUP * (g % 2 + 1))
@@ -121,36 +122,28 @@ def tile_transformerencoderblock_pa_kernel(tc, h_attn, x, masks, Wo, bo, out):
                 out=w_codes[:, cols].bitcast(E4M3), scales=w_scales[:, cols], in_=grouped[("w", pair)][:]
             )
 
-        mask_bank, mask_all = {}, {}
+        mask_all = {}
 
         def spread_mask(n):
-            mask_bank[n] = psum.tile([P, T], BF16, name="mask_bank", tag="turned", bufs=4)
+            bank = psum.tile([P, T], BF16, name="mask_bank", tag="bank")
             for h in range(2):
                 nc.tensor.matmul(
-                    mask_bank[n][:, HALF * h : HALF * (h + 1)],
+                    bank[:, HALF * h : HALF * (h + 1)],
                     lhsT=pick[:, h : h + 1].to_broadcast([P, P]),
                     rhs=first_rows[:] if n == 0 else later_rows[:, n - 1, :],
                     start=True,
                     stop=True,
                 )
             mask_all[n] = keep.tile([P, T], BF16, name="mask_all%d" % n)
-            nc.scalar.copy(out=mask_all[n][:], in_=mask_bank[n][:])
+            nc.scalar.copy(out=mask_all[n][:], in_=bank[:])
 
-        def turn_h(g, copy):
-            transpose(g, h_raw[g])
-            gather(g, copy, "h")
-
-        def turn_w(pair, copy):
-            transpose(("w", pair), w_raw[pair])
-            gather(("w", pair), copy, "w")
-
-        acc, masked, y, res = {}, {}, {}, {}
+        acc, masked, y, by_frame = {}, {}, {}, {}
         total, neg_mean, squares, rstd, shift = {}, {}, {}, {}, {}
 
         def project(i, h):
             n, j = divmod(i, SLOTS)
             cols = slice(P * j, P * (j + 1))
-            acc[i, h] = psum.tile([P, HALF], F32, name="acc", bufs=4)
+            acc[i, h] = psum.tile([P, HALF], F32, name="acc", tag="bank")
             nc.tensor.matmul_mx(
                 out=acc[i, h][:],
                 lhsT=w_codes[:, cols].bitcast(E4M3),
@@ -164,7 +157,7 @@ def tile_transformerencoderblock_pa_kernel(tc, h_attn, x, masks, Wo, bo, out):
         def bias_and_mask(i, h):
             n, j = divmod(i, SLOTS)
             if h == 0:
-                masked[i] = work.tile([P, T], F32, name="masked")
+                masked[i] = work.tile([P, T], F32, name="masked", bufs=TILES)
             cols = slice(HALF * h, HALF * (h + 1))
             nc.vector.scalar_tensor_tensor(
                 out=masked[i][:, cols], in0=acc[i, h][:], scalar=bias[:, j : j + 1],
@@ -172,105 +165,220 @@ def tile_transformerencoderblock_pa_kernel(tc, h_attn, x, masks, Wo, bo, out):
             )
 
         def add_residual(i):
-            y[i] = work.tile([P, T], F32, name="y", bufs=5)
+            y[i] = work.tile([P, T], F32, name="y", bufs=6)
             total[i] = stat.tile([P, 1], F32, name="total")
             nc.vector.scalar_tensor_tensor(
                 out=y[i][:], in0=masked[i][:], scalar=1.0, in1=x_sb[i][:],
                 op0=ALU.mult, op1=ALU.add, accum_out=total[i][:],
             )
-            if i in ON_VECTOR:
-                neg_mean[i] = stat.tile([P, 1], F32, name="neg_mean")
-                nc.gpsimd.tensor_scalar(
-                    out=neg_mean[i][:], in0=total[i][:], scalar1=-1.0 / T, scalar2=0.0, op0=ALU.mult, op1=ALU.add
-                )
+
+        def mean_scalar(i):
+            neg_mean[i] = stat.tile([P, 1], F32, name="neg_mean")
+            nc.scalar.activation(out=neg_mean[i][:], in_=total[i][:], func=ACT.Identity, scale=-1.0 / T)
 
         def sum_squares(i):
             squared = work.tile([P, T], BF16, name="squared", bufs=2)
             squares[i] = stat.tile([P, 1], F32, name="squares")
-            nc.scalar.activation(
-                out=squared[:], in_=y[i][:], func=ACT.Square, scale=-float(T), bias=total[i][:],
-                accum_out=squares[i][:],
-            )
+            if i < FIRST_LAST_TILE:
+                nc.scalar.activation(
+                    out=squared[:], in_=y[i][:], func=ACT.Square, scale=-float(T), bias=total[i][:],
+                    accum_out=squares[i][:],
+                )
+            else:
+                nc.scalar.activation(
+                    out=squared[:], in_=y[i][:], func=ACT.Square, bias=neg_mean[i][:], accum_out=squares[i][:]
+                )
 
         def inverse_std(i):
-            var = stat.tile([P, 1], F32, name="var")
-            nc.scalar.activation(out=var[:], in_=squares[i][:], func=ACT.Identity, scale=1.0 / T**3, bias=EPS)
             rstd[i] = stat.tile([P, 1], F32, name="rstd")
-            nc.gpsimd.tensor_tensor(out=rstd[i][:], in0=var[:], in1=minus_half[:], op=ALU.pow)
-            if i not in ON_VECTOR:
-                shift[i] = stat.tile([P, 1], F32, name="shift")
-                nc.gpsimd.tensor_scalar(
-                    out=shift[i][:], in0=total[i][:], scalar1=rstd[i][:], scalar2=-1.0 / T,
-                    op0=ALU.mult, op1=ALU.mult,
-                )
-
-        def normalise_scalar(i):
-            res[i] = work.tile([P, T], F32, name="res", bufs=TILES)
             nc.scalar.activation(
-                out=res[i][:], in_=y[i][:], func=ACT.Identity, scale=rstd[i][:], bias=shift[i][:],
+                out=rstd[i][:], in_=squares[i][:], func=ACT.Abs_reciprocal_sqrt,
+                scale=1.0 / T**3 if i < FIRST_LAST_TILE else 1.0 / T, bias=EPS,
             )
-            nc.sync.dma_start(out=out_rows[i // SLOTS, i % SLOTS], in_=res[i][:])
 
-        def normalise_vector(i, parts):
-            res[i] = work.tile([P, T], F32, name="res", bufs=TILES)
+        def normalise(i, engine, parts):
+            res = work.tile([P, T], F32, name="res", bufs=6)
             for h in range(parts):
                 cols = slice(T // parts * h, T // parts * (h + 1))
-                nc.vector.tensor_scalar(
-                    out=res[i][:, cols], in0=y[i][:, cols], scalar1=neg_mean[i][:], scalar2=rstd[i][:],
+                engine.tensor_scalar(
+                    out=res[:, cols], in0=y[i][:, cols], scalar1=neg_mean[i][:], scalar2=rstd[i][:],
                     op0=ALU.add, op1=ALU.mult,
                 )
-                nc.sync.dma_start(out=out_rows[i // SLOTS, i % SLOTS][:, cols], in_=res[i][:, cols])
+                nc.sync.dma_start(out=out_rows[i // SLOTS, i % SLOTS][:, cols], in_=res[:, cols])
+
+        def mean_vector(i):
+            shift[i] = stat.tile([P, 1], F32, name="shift")
+            nc.scalar.activation(out=shift[i][:], in_=neg_mean[i][:], func=ACT.Identity, scale=rstd[i][:])
+
+        def normalise_scalar(i):
+            pool_cols = POOL_COLS if i < POOL_TILES else 0
+            res = work.tile([P, T], F32, name="res", bufs=6)
+            nc.scalar.activation(
+                out=res[:, pool_cols:], in_=y[i][:, pool_cols:], func=ACT.Identity, scale=rstd[i][:], bias=shift[i][:]
+            )
+            nc.sync.dma_start(out=out_rows[i // SLOTS, i % SLOTS][:, pool_cols:], in_=res[:, pool_cols:])
+
+        def normalise_pool(i):
+            res = masked[i + 2]
+            nc.gpsimd.tensor_scalar(
+                out=res[:, :POOL_COLS], in0=y[i][:, :POOL_COLS], scalar1=neg_mean[i][:], scalar2=rstd[i][:],
+                op0=ALU.add, op1=ALU.mult,
+            )
+            nc.sync.dma_start(out=out_rows[i // SLOTS, i % SLOTS][:, :POOL_COLS], in_=res[:, :POOL_COLS])
 
         spread_mask(0)
-        turn_h(0, nc.vector.tensor_copy)
-        turn_w(0, nc.scalar.copy)
-        turn_h(1, nc.vector.tensor_copy)
-        turn_h(2, nc.scalar.copy)
-        turn_h(3, nc.scalar.copy)
+        turn_h(0, nc.scalar.copy)
+        turn_w(0, nc.vector.tensor_copy)
+        turn_h(1, nc.scalar.copy)
+        turn_h(2, nc.vector.tensor_copy)
         quantize_h(0)
+        turn_h(3, nc.scalar.copy)
         quantize_w(0)
         quantize_h(1)
-        project(0, 0)
-        project(1, 0)
         quantize_h(2)
+        turn_w(1, nc.scalar.copy)
+        project(0, 0)
         quantize_h(3)
         project(0, 1)
+        project(1, 0)
         project(1, 1)
-        turn_w(1, nc.scalar.copy)
         bias_and_mask(0, 0)
-        bias_and_mask(1, 0)
         bias_and_mask(0, 1)
         quantize_w(1)
+        add_residual(0)
         turn_h(4, nc.scalar.copy)
         project(2, 0)
-        add_residual(0)
-        turn_h(5, nc.scalar.copy)
+        bias_and_mask(1, 0)
         sum_squares(0)
+        mean_scalar(0)
+        turn_h(5, nc.scalar.copy)
         bias_and_mask(1, 1)
         quantize_h(4)
-
-        for i in range(2, TILES + 1):
-            if i < TILES:
-                bias_and_mask(i, 0)
-            if i + 3 < GROUPS:
-                quantize_h(i + 3)
-            if i < TILES:
-                project(i, 1)
-            if i + 4 < GROUPS:
-                turn_h(i + 4, nc.scalar.copy)
-            if i - 1 < N:
-                spread_mask(i - 1)
-            inverse_std(i - 2)
-            if i >= 3 and i - 3 not in ON_VECTOR:
-                normalise_scalar(i - 3)
-            add_residual(i - 1)
-            sum_squares(i - 1)
-            if i < TILES:
-                bias_and_mask(i, 1)
-            if i - 3 in ON_VECTOR:
-                normalise_vector(i - 3, 1)
-            if i + 1 < TILES:
-                project(i + 1, 0)
-        normalise_vector(TILES - 2, 1)
-        inverse_std(TILES - 1)
-        normalise_vector(TILES - 1, 2)
+        bias_and_mask(2, 0)
+        quantize_h(5)
+        project(2, 1)
+        turn_h(6, nc.scalar.copy)
+        inverse_std(0)
+        spread_mask(1)
+        mean_vector(0)
+        add_residual(1)
+        sum_squares(1)
+        mean_scalar(1)
+        bias_and_mask(2, 1)
+        project(3, 0)
+        bias_and_mask(3, 0)
+        quantize_h(6)
+        project(3, 1)
+        turn_h(7, nc.scalar.copy)
+        turn_h(8, nc.scalar.copy)
+        inverse_std(1)
+        normalise_scalar(0)
+        mean_vector(1)
+        add_residual(2)
+        normalise_pool(0)
+        sum_squares(2)
+        mean_scalar(2)
+        bias_and_mask(3, 1)
+        quantize_h(7)
+        project(4, 0)
+        bias_and_mask(4, 0)
+        quantize_h(8)
+        project(4, 1)
+        turn_h(9, nc.scalar.copy)
+        inverse_std(2)
+        normalise_scalar(1)
+        mean_vector(2)
+        add_residual(3)
+        normalise_pool(1)
+        sum_squares(3)
+        mean_scalar(3)
+        bias_and_mask(4, 1)
+        project(5, 0)
+        bias_and_mask(5, 0)
+        quantize_h(9)
+        project(5, 1)
+        turn_h(10, nc.scalar.copy)
+        inverse_std(3)
+        normalise_scalar(2)
+        mean_vector(3)
+        add_residual(4)
+        normalise_pool(2)
+        sum_squares(4)
+        mean_scalar(4)
+        bias_and_mask(5, 1)
+        project(6, 0)
+        bias_and_mask(6, 0)
+        quantize_h(10)
+        project(6, 1)
+        turn_h(11, nc.scalar.copy)
+        inverse_std(4)
+        normalise_scalar(3)
+        mean_vector(4)
+        add_residual(5)
+        normalise_pool(3)
+        sum_squares(5)
+        mean_scalar(5)
+        bias_and_mask(6, 1)
+        project(7, 0)
+        bias_and_mask(7, 0)
+        quantize_h(11)
+        project(7, 1)
+        inverse_std(5)
+        spread_mask(2)
+        normalise_scalar(4)
+        mean_vector(5)
+        add_residual(6)
+        normalise_pool(4)
+        sum_squares(6)
+        mean_scalar(6)
+        bias_and_mask(7, 1)
+        project(8, 0)
+        bias_and_mask(8, 0)
+        project(8, 1)
+        inverse_std(6)
+        normalise_scalar(5)
+        mean_vector(6)
+        add_residual(7)
+        normalise_pool(5)
+        sum_squares(7)
+        mean_scalar(7)
+        bias_and_mask(8, 1)
+        project(9, 0)
+        bias_and_mask(9, 0)
+        project(9, 1)
+        inverse_std(7)
+        normalise_scalar(6)
+        mean_vector(7)
+        add_residual(8)
+        normalise_pool(6)
+        sum_squares(8)
+        mean_scalar(8)
+        bias_and_mask(9, 1)
+        project(10, 0)
+        bias_and_mask(10, 0)
+        project(10, 1)
+        inverse_std(8)
+        normalise_scalar(7)
+        mean_vector(8)
+        add_residual(9)
+        normalise_pool(7)
+        sum_squares(9)
+        mean_scalar(9)
+        bias_and_mask(10, 1)
+        project(11, 0)
+        bias_and_mask(11, 0)
+        project(11, 1)
+        inverse_std(9)
+        normalise_scalar(8)
+        add_residual(10)
+        sum_squares(10)
+        mean_scalar(10)
+        bias_and_mask(11, 1)
+        normalise(9, nc.vector, 1)
+        inverse_std(10)
+        add_residual(11)
+        sum_squares(11)
+        mean_scalar(11)
+        normalise(10, nc.vector, 1)
+        inverse_std(11)
+        normalise(11, nc.vector, 2)

@@ -19,15 +19,15 @@ ACT = mybir.ActivationFunctionType
 P = 128
 HALF = 512
 GROUP = 256
+WORDS = C // 2
 SLOTS = E // P
 TILES = N * SLOTS
 GROUPS = N * T // GROUP
-BLOCKS = T // P
-POOL_COLS = 640
-POOL_TILES = 8
 LAST = N - 1
-FIRST_LAST_TILE = TILES
-FIRST_LAST_GROUP = LAST * T // GROUP
+LAST_TILES = LAST * SLOTS
+BLOCKS = HALF // P
+POOL_COLS = 640
+MASK_STEPS = {2: 1, 5: 2}
 
 
 def tile_transformerencoderblock_pa_kernel(tc, h_attn, x, masks, Wo, bo, out):
@@ -43,15 +43,16 @@ def tile_transformerencoderblock_pa_kernel(tc, h_attn, x, masks, Wo, bo, out):
         w_rows = Wo.rearrange("(p j) k -> p j k", j=SLOTS)
         x_rows = x.rearrange("n (p j) t -> n j p t", j=SLOTS)
         out_rows = out.rearrange("n (p j) t -> n j p t", j=SLOTS)
-
         mask_halves = masks.rearrange("n o (h t) -> (o h) n t", t=HALF)
-        first_rows = keep.tile([P, HALF], BF16, name="first_rows")
-        nc.gpsimd.memset(first_rows[:].bitcast(U32), 0)
-        nc.sync.dma_start(out=first_rows[0:2, :], in_=mask_halves[:, 0, :])
+
+        first_mask = keep.tile([P, HALF], BF16, name="first_mask")
+        nc.gpsimd.memset(first_mask[:].bitcast(U32), 0)
+        nc.sync.dma_start(out=first_mask[0:2, :], in_=mask_halves[:, 0, :])
         ident = keep.tile([P, P], F32, name="ident")
         make_identity(nc, ident[:])
-        later_rows = keep.tile([P, N - 1, HALF], BF16, name="later_rows")
+        later_rows = keep.tile([P, N, HALF], BF16, name="later_rows")
         nc.vector.memset(later_rows[:], 0.0)
+        last_mask, bias_row = later_rows[:, LAST - 1, :], later_rows[:, LAST, :]
         pick = keep.tile([P, 2], BF16, name="pick")
         nc.scalar.activation(out=pick[:], in_=ident[:, 0:2], func=ACT.Identity)
 
@@ -79,12 +80,14 @@ def tile_transformerencoderblock_pa_kernel(tc, h_attn, x, masks, Wo, bo, out):
         load_x(0)
         load_w(1)
         load_h(4)
-        for i in range(1, TILES):
+        load_h(5)
+        load_x(1)
+        nc.sync.dma_start(out=later_rows[0:2, :LAST], in_=mask_halves[:, 1:, :])
+        nc.sync.dma_start(out=later_rows[1:2, LAST], in_=bo.rearrange("(o e) -> o e", o=1))
+        for i in range(2, TILES):
             if i + 4 < GROUPS:
                 load_h(i + 4)
             load_x(i)
-            if i == 1:
-                nc.sync.dma_start(out=later_rows[0:2], in_=mask_halves[:, 1:, :])
 
         w_codes = keep.tile([P, E], U32, name="w_codes", align_bytes=64)
         w_scales = keep.tile([P, E], U8, name="w_scales", align_bytes=64)
@@ -93,51 +96,61 @@ def tile_transformerencoderblock_pa_kernel(tc, h_attn, x, masks, Wo, bo, out):
             h_codes[c] = keep.tile([P, HALF], U32, name="h_codes%d" % c, align_bytes=64)
             h_scales[c] = keep.tile([P, HALF], U8, name="h_scales%d" % c, align_bytes=64)
 
-        grouped = {}
-
-        def turn(key, raw, copy, src_order, dst_order):
+        def turn(raw, copy, bank_order, row_order):
             words = raw[:].rearrange("p j k -> p (j k)").bitcast(F32)
             bank = psum.tile([P, 2, 2, P], F32, name="turned", tag="bank")
             for j in range(2):
                 for u in range(2):
-                    nc.tensor.transpose(bank[:, j, u, :], words[:, 256 * j + u : 256 * (j + 1) : 2], ident[:])
-            grouped[key] = work.tile([P, 4 * GROUP], BF16, name="grouped", align_bytes=64, bufs=4)
-            copy(out=grouped[key][:].bitcast(F32).rearrange(dst_order, j=2, u=2), in_=bank[:].rearrange(src_order))
+                    nc.tensor.transpose(bank[:, j, u, :], words[:, WORDS * j + u : WORDS * (j + 1) : 2], ident[:])
+            quads = work.tile([P, 4 * GROUP], BF16, name="quads", align_bytes=64, bufs=4)
+            copy(out=quads[:].bitcast(F32).rearrange(row_order, j=2, u=2), in_=bank[:].rearrange(bank_order))
+            return quads
+
+        h_quads, w_quads = {}, {}
 
         def turn_h(g, copy):
-            turn(g, h_raw[g], copy, "p j u r -> p r j u", "p (r j u) -> p r j u")
+            h_quads[g] = turn(h_raw[g], copy, "p j u r -> p r j u", "p (r j u) -> p r j u")
 
         def turn_w(pair, copy):
-            turn(("w", pair), w_raw[pair], copy, "p j u r -> p j r u", "p (j r u) -> p j r u")
+            w_quads[pair] = turn(w_raw[pair], copy, "p j u r -> p j r u", "p (j r u) -> p j r u")
 
         def quantize_h(g):
             cols = slice(GROUP * (g % 2), GROUP * (g % 2 + 1))
             nc.vector.quantize_mx(
-                out=h_codes[g // 2][:, cols].bitcast(E5M2), scales=h_scales[g // 2][:, cols], in_=grouped[g][:]
+                out=h_codes[g // 2][:, cols].bitcast(E5M2), scales=h_scales[g // 2][:, cols], in_=h_quads[g][:]
             )
 
         def quantize_w(pair):
-            cols = slice(2 * P * pair, 2 * P * (pair + 1))
-            nc.vector.quantize_mx(
-                out=w_codes[:, cols].bitcast(E4M3), scales=w_scales[:, cols], in_=grouped[("w", pair)][:]
-            )
+            cols = slice(GROUP * pair, GROUP * (pair + 1))
+            nc.vector.quantize_mx(out=w_codes[:, cols].bitcast(E4M3), scales=w_scales[:, cols], in_=w_quads[pair][:])
 
         mask_all = {}
 
         def spread_mask(n):
-            bank = psum.tile([P, T], BF16, name="mask_bank", tag="bank")
-            for h in range(2):
+            halves = 1 if n == LAST else 2
+            bank = psum.tile([P, halves * HALF], BF16, name="mask_bank", tag="bank")
+            for h in range(halves):
                 nc.tensor.matmul(
                     bank[:, HALF * h : HALF * (h + 1)],
                     lhsT=pick[:, h : h + 1].to_broadcast([P, P]),
-                    rhs=first_rows[:] if n == 0 else later_rows[:, n - 1, :],
+                    rhs=first_mask[:] if n == 0 else later_rows[:, n - 1, :],
                     start=True,
                     stop=True,
                 )
-            mask_all[n] = keep.tile([P, T], BF16, name="mask_all%d" % n)
+            mask_all[n] = keep.tile([P, halves * HALF], BF16, name="mask_all%d" % n)
             nc.scalar.copy(out=mask_all[n][:], in_=bank[:])
 
-        acc, masked, y, by_frame = {}, {}, {}, {}
+        frame_mask = keep.tile([P, BLOCKS], F32, name="frame_mask")
+
+        def mask_by_frame():
+            bank = psum.tile([P, BLOCKS, 2], F32, name="mask_turned", tag="bank")
+            for b in range(BLOCKS):
+                nc.tensor.matmul(
+                    bank[:, b, :], lhsT=last_mask[:, P * b : P * (b + 1)], rhs=pick[:], start=True, stop=True
+                )
+            nc.scalar.copy(out=frame_mask[:], in_=bank[:, :, 1])
+
+        acc, by_frame, masked, y = {}, {}, {}, {}
         total, neg_mean, squares, rstd, shift = {}, {}, {}, {}, {}
 
         def project(i, h):
@@ -154,6 +167,36 @@ def tile_transformerencoderblock_pa_kernel(tc, h_attn, x, masks, Wo, bo, out):
                 stop=True,
             )
 
+        def project_by_frame(g):
+            for b in range(2 * (g % 2), 2 * (g % 2) + 2):
+                cols = slice(P * b, P * (b + 1))
+                bank = psum.tile([P, E], F32, name="frames", tag="bank")
+                nc.tensor.matmul_mx(
+                    out=bank[:],
+                    lhsT=h_codes[g // 2][:, cols].bitcast(E5M2),
+                    lhsT_scale=h_scales[g // 2][:, cols],
+                    rhs=w_codes[:].bitcast(E4M3),
+                    rhs_scale=w_scales[:],
+                    start=True,
+                    stop=True,
+                )
+                by_frame[b] = keep.tile([P, E], F32, name="by_frame%d" % b)
+                nc.scalar.activation(out=by_frame[b][:], in_=bank[:], func=ACT.Identity, scale=frame_mask[:, b : b + 1])
+
+        def bring_back(i):
+            j = i % SLOTS
+            acc[i, 1] = psum.tile([P, HALF], F32, name="acc", tag="bank")
+            nc.tensor.matmul(acc[i, 1][:], lhsT=bias_row[:, j::SLOTS], rhs=last_mask, start=True, stop=False)
+            for b in range(BLOCKS):
+                nc.tensor.matmul(
+                    acc[i, 1][:, P * b : P * (b + 1)],
+                    lhsT=by_frame[b][:, P * j : P * (j + 1)],
+                    rhs=ident[:],
+                    is_transpose=True,
+                    start=False,
+                    stop=(b == BLOCKS - 1),
+                )
+
         def bias_and_mask(i, h):
             n, j = divmod(i, SLOTS)
             if h == 0:
@@ -164,67 +207,87 @@ def tile_transformerencoderblock_pa_kernel(tc, h_attn, x, masks, Wo, bo, out):
                 in1=mask_all[n][:, cols], op0=ALU.add, op1=ALU.mult,
             )
 
+        def y_tile():
+            return work.tile([P, T], F32, name="y", bufs=6)
+
         def add_residual(i):
-            y[i] = work.tile([P, T], F32, name="y", bufs=6)
+            y[i] = y_tile()
             total[i] = stat.tile([P, 1], F32, name="total")
             nc.vector.scalar_tensor_tensor(
                 out=y[i][:], in0=masked[i][:], scalar=1.0, in1=x_sb[i][:],
                 op0=ALU.mult, op1=ALU.add, accum_out=total[i][:],
             )
 
-        def mean_scalar(i):
+        def add_residual_half(i, h):
+            if h == 1:
+                y[i] = y_tile()
+                total[i] = stat.tile([P, 2], F32, name="total")
+            cols = slice(HALF * h, HALF * (h + 1))
+            nc.vector.scalar_tensor_tensor(
+                out=y[i][:, cols], in0=acc[i, 1][:] if h == 1 else masked[i][:, cols], scalar=1.0,
+                in1=x_sb[i][:, cols], op0=ALU.mult, op1=ALU.add, accum_out=total[i][:, h : h + 1],
+            )
+
+        def mean_of_halves(i):
+            neg_mean[i] = stat.tile([P, 1], F32, name="neg_mean")
+            nc.vector.tensor_scalar(
+                out=neg_mean[i][:], in0=total[i][:, 0:1], scalar1=total[i][:, 1:2], scalar2=-1.0 / T,
+                op0=ALU.add, op1=ALU.mult,
+            )
+
+        def sum_squares(i, scale, offset):
+            squared = work.tile([P, T], BF16, name="squared", bufs=2)
+            squares[i] = stat.tile([P, 1], F32, name="squares")
+            nc.scalar.activation(
+                out=squared[:], in_=y[i][:], func=ACT.Square, scale=scale, bias=offset[:], accum_out=squares[i][:]
+            )
+
+        def moments(i):
+            sum_squares(i, -float(T), total[i])
             neg_mean[i] = stat.tile([P, 1], F32, name="neg_mean")
             nc.scalar.activation(out=neg_mean[i][:], in_=total[i][:], func=ACT.Identity, scale=-1.0 / T)
 
-        def sum_squares(i):
-            squared = work.tile([P, T], BF16, name="squared", bufs=2)
-            squares[i] = stat.tile([P, 1], F32, name="squares")
-            if i < FIRST_LAST_TILE:
-                nc.scalar.activation(
-                    out=squared[:], in_=y[i][:], func=ACT.Square, scale=-float(T), bias=total[i][:],
-                    accum_out=squares[i][:],
-                )
-            else:
-                nc.scalar.activation(
-                    out=squared[:], in_=y[i][:], func=ACT.Square, bias=neg_mean[i][:], accum_out=squares[i][:]
-                )
-
         def inverse_std(i):
+            to_variance = 1.0 / T**3 if i < LAST_TILES else 1.0 / T
             rstd[i] = stat.tile([P, 1], F32, name="rstd")
             nc.scalar.activation(
-                out=rstd[i][:], in_=squares[i][:], func=ACT.Abs_reciprocal_sqrt,
-                scale=1.0 / T**3 if i < FIRST_LAST_TILE else 1.0 / T, bias=EPS,
+                out=rstd[i][:], in_=squares[i][:], func=ACT.Abs_reciprocal_sqrt, scale=to_variance, bias=EPS
             )
 
-        def normalise(i, engine, parts):
-            res = work.tile([P, T], F32, name="res", bufs=6)
-            for h in range(parts):
-                cols = slice(T // parts * h, T // parts * (h + 1))
-                engine.tensor_scalar(
-                    out=res[:, cols], in0=y[i][:, cols], scalar1=neg_mean[i][:], scalar2=rstd[i][:],
-                    op0=ALU.add, op1=ALU.mult,
-                )
-                nc.sync.dma_start(out=out_rows[i // SLOTS, i % SLOTS][:, cols], in_=res[:, cols])
-
-        def mean_vector(i):
+        def mean_shift(i):
             shift[i] = stat.tile([P, 1], F32, name="shift")
             nc.scalar.activation(out=shift[i][:], in_=neg_mean[i][:], func=ACT.Identity, scale=rstd[i][:])
 
-        def normalise_scalar(i):
-            pool_cols = POOL_COLS if i < POOL_TILES else 0
-            res = work.tile([P, T], F32, name="res", bufs=6)
-            nc.scalar.activation(
-                out=res[:, pool_cols:], in_=y[i][:, pool_cols:], func=ACT.Identity, scale=rstd[i][:], bias=shift[i][:]
-            )
-            nc.sync.dma_start(out=out_rows[i // SLOTS, i % SLOTS][:, pool_cols:], in_=res[:, pool_cols:])
+        def store(i, cols, res):
+            nc.sync.dma_start(out=out_rows[i // SLOTS, i % SLOTS][:, cols], in_=res[:, cols])
 
-        def normalise_pool(i):
-            res = masked[i + 2]
+        def result_tile():
+            return work.tile([P, T], F32, name="res", bufs=6)
+
+        def normalise_scalar(i, first_col):
+            res, cols = result_tile(), slice(first_col, T)
+            nc.scalar.activation(
+                out=res[:, cols], in_=y[i][:, cols], func=ACT.Identity, scale=rstd[i][:], bias=shift[i][:]
+            )
+            store(i, cols, res)
+
+        def normalise_pool(i, end_col):
+            res, cols = masked[i + 2], slice(0, end_col)
             nc.gpsimd.tensor_scalar(
-                out=res[:, :POOL_COLS], in0=y[i][:, :POOL_COLS], scalar1=neg_mean[i][:], scalar2=rstd[i][:],
+                out=res[:, cols], in0=y[i][:, cols], scalar1=neg_mean[i][:], scalar2=rstd[i][:],
                 op0=ALU.add, op1=ALU.mult,
             )
-            nc.sync.dma_start(out=out_rows[i // SLOTS, i % SLOTS][:, :POOL_COLS], in_=res[:, :POOL_COLS])
+            store(i, cols, res)
+
+        def normalise_vector(i, parts):
+            res = result_tile()
+            for h in range(parts):
+                cols = slice(T // parts * h, T // parts * (h + 1))
+                nc.vector.tensor_scalar(
+                    out=res[:, cols], in0=y[i][:, cols], scalar1=neg_mean[i][:], scalar2=rstd[i][:],
+                    op0=ALU.add, op1=ALU.mult,
+                )
+                store(i, cols, res)
 
         spread_mask(0)
         turn_h(0, nc.scalar.copy)
@@ -249,136 +312,76 @@ def tile_transformerencoderblock_pa_kernel(tc, h_attn, x, masks, Wo, bo, out):
         turn_h(4, nc.scalar.copy)
         project(2, 0)
         bias_and_mask(1, 0)
-        sum_squares(0)
-        mean_scalar(0)
+        moments(0)
         turn_h(5, nc.scalar.copy)
         bias_and_mask(1, 1)
         quantize_h(4)
-        bias_and_mask(2, 0)
-        quantize_h(5)
-        project(2, 1)
-        turn_h(6, nc.scalar.copy)
-        inverse_std(0)
-        spread_mask(1)
-        mean_vector(0)
-        add_residual(1)
-        sum_squares(1)
-        mean_scalar(1)
-        bias_and_mask(2, 1)
-        project(3, 0)
-        bias_and_mask(3, 0)
-        quantize_h(6)
-        project(3, 1)
-        turn_h(7, nc.scalar.copy)
-        turn_h(8, nc.scalar.copy)
-        inverse_std(1)
-        normalise_scalar(0)
-        mean_vector(1)
-        add_residual(2)
-        normalise_pool(0)
-        sum_squares(2)
-        mean_scalar(2)
-        bias_and_mask(3, 1)
-        quantize_h(7)
-        project(4, 0)
-        bias_and_mask(4, 0)
-        quantize_h(8)
-        project(4, 1)
-        turn_h(9, nc.scalar.copy)
-        inverse_std(2)
-        normalise_scalar(1)
-        mean_vector(2)
-        add_residual(3)
-        normalise_pool(1)
-        sum_squares(3)
-        mean_scalar(3)
-        bias_and_mask(4, 1)
-        project(5, 0)
-        bias_and_mask(5, 0)
-        quantize_h(9)
-        project(5, 1)
-        turn_h(10, nc.scalar.copy)
-        inverse_std(3)
-        normalise_scalar(2)
-        mean_vector(3)
-        add_residual(4)
-        normalise_pool(2)
-        sum_squares(4)
-        mean_scalar(4)
-        bias_and_mask(5, 1)
-        project(6, 0)
-        bias_and_mask(6, 0)
-        quantize_h(10)
-        project(6, 1)
-        turn_h(11, nc.scalar.copy)
-        inverse_std(4)
-        normalise_scalar(3)
-        mean_vector(4)
-        add_residual(5)
-        normalise_pool(3)
-        sum_squares(5)
-        mean_scalar(5)
-        bias_and_mask(6, 1)
-        project(7, 0)
-        bias_and_mask(7, 0)
-        quantize_h(11)
-        project(7, 1)
-        inverse_std(5)
-        spread_mask(2)
-        normalise_scalar(4)
-        mean_vector(5)
-        add_residual(6)
-        normalise_pool(4)
-        sum_squares(6)
-        mean_scalar(6)
-        bias_and_mask(7, 1)
-        project(8, 0)
-        bias_and_mask(8, 0)
-        project(8, 1)
-        inverse_std(6)
-        normalise_scalar(5)
-        mean_vector(6)
-        add_residual(7)
-        normalise_pool(5)
-        sum_squares(7)
-        mean_scalar(7)
-        bias_and_mask(8, 1)
-        project(9, 0)
-        bias_and_mask(9, 0)
-        project(9, 1)
-        inverse_std(7)
-        normalise_scalar(6)
-        mean_vector(7)
-        add_residual(8)
-        normalise_pool(6)
-        sum_squares(8)
-        mean_scalar(8)
-        bias_and_mask(9, 1)
-        project(10, 0)
-        bias_and_mask(10, 0)
-        project(10, 1)
-        inverse_std(8)
-        normalise_scalar(7)
-        mean_vector(8)
-        add_residual(9)
-        normalise_pool(7)
-        sum_squares(9)
-        mean_scalar(9)
-        bias_and_mask(10, 1)
-        project(11, 0)
-        bias_and_mask(11, 0)
-        project(11, 1)
-        inverse_std(9)
-        normalise_scalar(8)
-        add_residual(10)
-        sum_squares(10)
-        mean_scalar(10)
-        bias_and_mask(11, 1)
-        normalise(9, nc.vector, 1)
-        inverse_std(10)
-        add_residual(11)
-        sum_squares(11)
-        mean_scalar(11)
-        normalise(10, nc.vector, 1)
-        inverse_std(11)
-        normalise(11, nc.vector, 2)
+
+        whole_on_pool = (LAST_TILES - 4, LAST_TILES - 3)
+        for i in range(2, LAST_TILES):
+            bias_and_mask(i, 0)
+            g = i + 3 if i < SLOTS else i + 4
+            quantize_h(g)
+            project(i, 1)
+            if i < SLOTS:
+                turn_h(i + 4, nc.scalar.copy)
+            if SLOTS - 1 <= i < GROUPS - 5:
+                turn_h(i + 5, nc.scalar.copy)
+            if g >= GROUPS - 2:
+                project_by_frame(g)
+            if MASK_STEPS.get(i) == LAST:
+                mask_by_frame()
+                spread_mask(LAST)
+            inverse_std(i - 2)
+            if MASK_STEPS.get(i) == 1:
+                spread_mask(1)
+            if i >= 3 and i - 3 not in whole_on_pool:
+                normalise_scalar(i - 3, POOL_COLS)
+            if i - 2 not in whole_on_pool:
+                mean_shift(i - 2)
+            add_residual(i - 1)
+            if i >= 3:
+                normalise_pool(i - 3, T if i - 3 in whole_on_pool else POOL_COLS)
+            moments(i - 1)
+            bias_and_mask(i, 1)
+            if i == SLOTS - 1:
+                quantize_h(i + 4)
+            project(i + 1, 0)
+
+        first, last = LAST_TILES, TILES - 1
+        project(first + 1, 0)
+        bring_back(first)
+        bias_and_mask(first, 0)
+        inverse_std(first - 2)
+        mean_shift(first - 2)
+        add_residual(first - 1)
+        normalise_pool(first - 3, T)
+        moments(first - 1)
+
+        for i in range(first, last):
+            add_residual_half(i, 1)
+            if i > first:
+                mean_of_halves(i - 1)
+                project(i + 1, 0)
+            bring_back(i + 1)
+            if i > first:
+                sum_squares(i - 1, 1.0, neg_mean[i - 1])
+            bias_and_mask(i + 1, 0)
+            add_residual_half(i, 0)
+            normalise_scalar(i - 2, HALF)
+            normalise_pool(i - 2, HALF)
+            inverse_std(i - 1)
+            if i + 1 < last:
+                mean_shift(i - 1)
+
+        add_residual_half(last, 1)
+        mean_of_halves(last - 1)
+        sum_squares(last - 1, 1.0, neg_mean[last - 1])
+        add_residual_half(last, 0)
+        normalise_vector(last - 2, 1)
+        mean_of_halves(last)
+        inverse_std(last - 1)
+        sum_squares(last, 1.0, neg_mean[last])
+        normalise_vector(last - 1, 1)
+        inverse_std(last)
+        normalise_vector(last, 2)

from contextlib import ExitStack

import concourse.mybir as mybir
from concourse.masks import make_identity

N, T, C, E = 3, 1024, 512, 512
EPS = 1e-5
FLOPS = 2 * N * T * C * E

F32 = mybir.dt.float32
BF16 = mybir.dt.bfloat16
U32 = mybir.dt.uint32
U8 = mybir.dt.uint8
E4M3 = mybir.dt.float8_e4m3fn_x4
E5M2 = mybir.dt.float8_e5m2_x4
ALU = mybir.AluOpType
ACT = mybir.ActivationFunctionType

P = 128
HALF = 512
GROUP = 256
WORDS = C // 2
SLOTS = E // P
TILES = N * SLOTS
GROUPS = N * T // GROUP
LAST = N - 1
LAST_TILES = LAST * SLOTS
BLOCKS = HALF // P
POOL_COLS = 640
MASK_STEPS = {2: 1, 5: 2}


def tile_transformerencoderblock_pa_kernel(tc, h_attn, x, masks, Wo, bo, out):
    nc = tc.nc
    with ExitStack() as ctx:
        keep = ctx.enter_context(tc.tile_pool(name="keep", bufs=1))
        work = ctx.enter_context(tc.tile_pool(name="work", bufs=3))
        stat = ctx.enter_context(tc.tile_pool(name="stat", bufs=TILES))
        psum = ctx.enter_context(tc.psum_pool(name="psum", bufs=8))
        ctx.enter_context(tc.manual_schedule())

        h_rows = h_attn.rearrange("n (g p j) k -> (n g) p j k", p=P, j=2)
        w_rows = Wo.rearrange("(p j) k -> p j k", j=SLOTS)
        x_rows = x.rearrange("n (p j) t -> n j p t", j=SLOTS)
        out_rows = out.rearrange("n (p j) t -> n j p t", j=SLOTS)
        mask_halves = masks.rearrange("n o (h t) -> (o h) n t", t=HALF)

        first_mask = keep.tile([P, HALF], BF16, name="first_mask")
        nc.gpsimd.memset(first_mask[:].bitcast(U32), 0)
        nc.sync.dma_start(out=first_mask[0:2, :], in_=mask_halves[:, 0, :])
        ident = keep.tile([P, P], F32, name="ident")
        make_identity(nc, ident[:])
        later_rows = keep.tile([P, N, HALF], BF16, name="later_rows")
        nc.vector.memset(later_rows[:], 0.0)
        last_mask, bias_row = later_rows[:, LAST - 1, :], later_rows[:, LAST, :]
        pick = keep.tile([P, 2], BF16, name="pick")
        nc.scalar.activation(out=pick[:], in_=ident[:, 0:2], func=ACT.Identity)

        h_raw, w_raw, x_sb = {}, {}, {}

        def load_h(g):
            h_raw[g] = keep.tile([P, 2, C], BF16, name="h_raw%d" % g)
            nc.sync.dma_start(out=h_raw[g][:], in_=h_rows[g])

        def load_w(pair):
            w_raw[pair] = keep.tile([P, 2, C], BF16, name="w_raw%d" % pair)
            nc.sync.dma_start(out=w_raw[pair][:], in_=w_rows[:, 2 * pair : 2 * pair + 2, :])

        def load_x(i):
            x_sb[i] = keep.tile([P, T], BF16, name="x_sb%d" % i)
            nc.sync.dma_start(out=x_sb[i][:], in_=x_rows[i // SLOTS, i % SLOTS])

        load_h(0)
        load_w(0)
        load_h(1)
        load_h(2)
        load_h(3)
        bias = keep.tile([P, SLOTS], BF16, name="bias")
        nc.sync.dma_start(out=bias[:], in_=bo.rearrange("(p j) -> p j", j=SLOTS))
        load_x(0)
        load_w(1)
        load_h(4)
        load_h(5)
        load_x(1)
        nc.sync.dma_start(out=later_rows[0:2, :LAST], in_=mask_halves[:, 1:, :])
        nc.sync.dma_start(out=later_rows[1:2, LAST], in_=bo.rearrange("(o e) -> o e", o=1))
        for i in range(2, TILES):
            if i + 4 < GROUPS:
                load_h(i + 4)
            load_x(i)

        w_codes = keep.tile([P, E], U32, name="w_codes", align_bytes=64)
        w_scales = keep.tile([P, E], U8, name="w_scales", align_bytes=64)
        h_codes, h_scales = {}, {}
        for c in range(N * T // HALF):
            h_codes[c] = keep.tile([P, HALF], U32, name="h_codes%d" % c, align_bytes=64)
            h_scales[c] = keep.tile([P, HALF], U8, name="h_scales%d" % c, align_bytes=64)

        def turn(raw, copy, bank_order, row_order):
            words = raw[:].rearrange("p j k -> p (j k)").bitcast(F32)
            bank = psum.tile([P, 2, 2, P], F32, name="turned", tag="bank")
            for j in range(2):
                for u in range(2):
                    nc.tensor.transpose(bank[:, j, u, :], words[:, WORDS * j + u : WORDS * (j + 1) : 2], ident[:])
            quads = work.tile([P, 4 * GROUP], BF16, name="quads", align_bytes=64, bufs=4)
            copy(out=quads[:].bitcast(F32).rearrange(row_order, j=2, u=2), in_=bank[:].rearrange(bank_order))
            return quads

        h_quads, w_quads = {}, {}

        def turn_h(g, copy):
            h_quads[g] = turn(h_raw[g], copy, "p j u r -> p r j u", "p (r j u) -> p r j u")

        def turn_w(pair, copy):
            w_quads[pair] = turn(w_raw[pair], copy, "p j u r -> p j r u", "p (j r u) -> p j r u")

        def quantize_h(g):
            cols = slice(GROUP * (g % 2), GROUP * (g % 2 + 1))
            nc.vector.quantize_mx(
                out=h_codes[g // 2][:, cols].bitcast(E5M2), scales=h_scales[g // 2][:, cols], in_=h_quads[g][:]
            )

        def quantize_w(pair):
            cols = slice(GROUP * pair, GROUP * (pair + 1))
            nc.vector.quantize_mx(out=w_codes[:, cols].bitcast(E4M3), scales=w_scales[:, cols], in_=w_quads[pair][:])

        mask_all = {}

        def spread_mask(n):
            halves = 1 if n == LAST else 2
            bank = psum.tile([P, halves * HALF], BF16, name="mask_bank", tag="bank")
            for h in range(halves):
                nc.tensor.matmul(
                    bank[:, HALF * h : HALF * (h + 1)],
                    lhsT=pick[:, h : h + 1].to_broadcast([P, P]),
                    rhs=first_mask[:] if n == 0 else later_rows[:, n - 1, :],
                    start=True,
                    stop=True,
                )
            mask_all[n] = keep.tile([P, halves * HALF], BF16, name="mask_all%d" % n)
            nc.scalar.copy(out=mask_all[n][:], in_=bank[:])

        frame_mask = keep.tile([P, BLOCKS], F32, name="frame_mask")

        def mask_by_frame():
            bank = psum.tile([P, BLOCKS, 2], F32, name="mask_turned", tag="bank")
            for b in range(BLOCKS):
                nc.tensor.matmul(
                    bank[:, b, :], lhsT=last_mask[:, P * b : P * (b + 1)], rhs=pick[:], start=True, stop=True
                )
            nc.scalar.copy(out=frame_mask[:], in_=bank[:, :, 1])

        acc, by_frame, masked, y = {}, {}, {}, {}
        total, neg_mean, squares, rstd, shift = {}, {}, {}, {}, {}

        def project(i, h):
            n, j = divmod(i, SLOTS)
            cols = slice(P * j, P * (j + 1))
            acc[i, h] = psum.tile([P, HALF], F32, name="acc", tag="bank")
            nc.tensor.matmul_mx(
                out=acc[i, h][:],
                lhsT=w_codes[:, cols].bitcast(E4M3),
                lhsT_scale=w_scales[:, cols],
                rhs=h_codes[2 * n + h][:].bitcast(E5M2),
                rhs_scale=h_scales[2 * n + h][:],
                start=True,
                stop=True,
            )

        def project_by_frame(g):
            for b in range(2 * (g % 2), 2 * (g % 2) + 2):
                cols = slice(P * b, P * (b + 1))
                bank = psum.tile([P, E], F32, name="frames", tag="bank")
                nc.tensor.matmul_mx(
                    out=bank[:],
                    lhsT=h_codes[g // 2][:, cols].bitcast(E5M2),
                    lhsT_scale=h_scales[g // 2][:, cols],
                    rhs=w_codes[:].bitcast(E4M3),
                    rhs_scale=w_scales[:],
                    start=True,
                    stop=True,
                )
                by_frame[b] = keep.tile([P, E], F32, name="by_frame%d" % b)
                nc.scalar.activation(out=by_frame[b][:], in_=bank[:], func=ACT.Identity, scale=frame_mask[:, b : b + 1])

        def bring_back(i):
            j = i % SLOTS
            acc[i, 1] = psum.tile([P, HALF], F32, name="acc", tag="bank")
            nc.tensor.matmul(acc[i, 1][:], lhsT=bias_row[:, j::SLOTS], rhs=last_mask, start=True, stop=False)
            for b in range(BLOCKS):
                nc.tensor.matmul(
                    acc[i, 1][:, P * b : P * (b + 1)],
                    lhsT=by_frame[b][:, P * j : P * (j + 1)],
                    rhs=ident[:],
                    is_transpose=True,
                    start=False,
                    stop=(b == BLOCKS - 1),
                )

        def bias_and_mask(i, h):
            n, j = divmod(i, SLOTS)
            if h == 0:
                masked[i] = work.tile([P, T], F32, name="masked", bufs=TILES)
            cols = slice(HALF * h, HALF * (h + 1))
            nc.vector.scalar_tensor_tensor(
                out=masked[i][:, cols], in0=acc[i, h][:], scalar=bias[:, j : j + 1],
                in1=mask_all[n][:, cols], op0=ALU.add, op1=ALU.mult,
            )

        def y_tile():
            return work.tile([P, T], F32, name="y", bufs=6)

        def add_residual(i):
            y[i] = y_tile()
            total[i] = stat.tile([P, 1], F32, name="total")
            nc.vector.scalar_tensor_tensor(
                out=y[i][:], in0=masked[i][:], scalar=1.0, in1=x_sb[i][:],
                op0=ALU.mult, op1=ALU.add, accum_out=total[i][:],
            )

        def add_residual_half(i, h):
            if h == 1:
                y[i] = y_tile()
                total[i] = stat.tile([P, 2], F32, name="total")
            cols = slice(HALF * h, HALF * (h + 1))
            nc.vector.scalar_tensor_tensor(
                out=y[i][:, cols], in0=acc[i, 1][:] if h == 1 else masked[i][:, cols], scalar=1.0,
                in1=x_sb[i][:, cols], op0=ALU.mult, op1=ALU.add, accum_out=total[i][:, h : h + 1],
            )

        def mean_of_halves(i):
            neg_mean[i] = stat.tile([P, 1], F32, name="neg_mean")
            nc.vector.tensor_scalar(
                out=neg_mean[i][:], in0=total[i][:, 0:1], scalar1=total[i][:, 1:2], scalar2=-1.0 / T,
                op0=ALU.add, op1=ALU.mult,
            )

        def sum_squares(i, scale, offset):
            squared = work.tile([P, T], BF16, name="squared", bufs=2)
            squares[i] = stat.tile([P, 1], F32, name="squares")
            nc.scalar.activation(
                out=squared[:], in_=y[i][:], func=ACT.Square, scale=scale, bias=offset[:], accum_out=squares[i][:]
            )

        def moments(i):
            sum_squares(i, -float(T), total[i])
            neg_mean[i] = stat.tile([P, 1], F32, name="neg_mean")
            nc.scalar.activation(out=neg_mean[i][:], in_=total[i][:], func=ACT.Identity, scale=-1.0 / T)

        def inverse_std(i):
            to_variance = 1.0 / T**3 if i < LAST_TILES else 1.0 / T
            rstd[i] = stat.tile([P, 1], F32, name="rstd")
            nc.scalar.activation(
                out=rstd[i][:], in_=squares[i][:], func=ACT.Abs_reciprocal_sqrt, scale=to_variance, bias=EPS
            )

        def mean_shift(i):
            shift[i] = stat.tile([P, 1], F32, name="shift")
            nc.scalar.activation(out=shift[i][:], in_=neg_mean[i][:], func=ACT.Identity, scale=rstd[i][:])

        def store(i, cols, res):
            nc.sync.dma_start(out=out_rows[i // SLOTS, i % SLOTS][:, cols], in_=res[:, cols])

        def result_tile():
            return work.tile([P, T], F32, name="res", bufs=6)

        def normalise_scalar(i, first_col):
            res, cols = result_tile(), slice(first_col, T)
            nc.scalar.activation(
                out=res[:, cols], in_=y[i][:, cols], func=ACT.Identity, scale=rstd[i][:], bias=shift[i][:]
            )
            store(i, cols, res)

        def normalise_pool(i, end_col):
            res, cols = masked[i + 2], slice(0, end_col)
            nc.gpsimd.tensor_scalar(
                out=res[:, cols], in0=y[i][:, cols], scalar1=neg_mean[i][:], scalar2=rstd[i][:],
                op0=ALU.add, op1=ALU.mult,
            )
            store(i, cols, res)

        def normalise_vector(i, parts):
            res = result_tile()
            for h in range(parts):
                cols = slice(T // parts * h, T // parts * (h + 1))
                nc.vector.tensor_scalar(
                    out=res[:, cols], in0=y[i][:, cols], scalar1=neg_mean[i][:], scalar2=rstd[i][:],
                    op0=ALU.add, op1=ALU.mult,
                )
                store(i, cols, res)

        spread_mask(0)
        turn_h(0, nc.scalar.copy)
        turn_w(0, nc.vector.tensor_copy)
        turn_h(1, nc.scalar.copy)
        turn_h(2, nc.vector.tensor_copy)
        quantize_h(0)
        turn_h(3, nc.scalar.copy)
        quantize_w(0)
        quantize_h(1)
        quantize_h(2)
        turn_w(1, nc.scalar.copy)
        project(0, 0)
        quantize_h(3)
        project(0, 1)
        project(1, 0)
        project(1, 1)
        bias_and_mask(0, 0)
        bias_and_mask(0, 1)
        quantize_w(1)
        add_residual(0)
        turn_h(4, nc.scalar.copy)
        project(2, 0)
        bias_and_mask(1, 0)
        moments(0)
        turn_h(5, nc.scalar.copy)
        bias_and_mask(1, 1)
        quantize_h(4)

        whole_on_pool = (LAST_TILES - 4, LAST_TILES - 3)
        for i in range(2, LAST_TILES):
            bias_and_mask(i, 0)
            g = i + 3 if i < SLOTS else i + 4
            quantize_h(g)
            project(i, 1)
            if i < SLOTS:
                turn_h(i + 4, nc.scalar.copy)
            if SLOTS - 1 <= i < GROUPS - 5:
                turn_h(i + 5, nc.scalar.copy)
            if g >= GROUPS - 2:
                project_by_frame(g)
            if MASK_STEPS.get(i) == LAST:
                mask_by_frame()
                spread_mask(LAST)
            inverse_std(i - 2)
            if MASK_STEPS.get(i) == 1:
                spread_mask(1)
            if i >= 3 and i - 3 not in whole_on_pool:
                normalise_scalar(i - 3, POOL_COLS)
            if i - 2 not in whole_on_pool:
                mean_shift(i - 2)
            add_residual(i - 1)
            if i >= 3:
                normalise_pool(i - 3, T if i - 3 in whole_on_pool else POOL_COLS)
            moments(i - 1)
            bias_and_mask(i, 1)
            if i == SLOTS - 1:
                quantize_h(i + 4)
            project(i + 1, 0)

        first, last = LAST_TILES, TILES - 1
        project(first + 1, 0)
        bring_back(first)
        bias_and_mask(first, 0)
        inverse_std(first - 2)
        mean_shift(first - 2)
        add_residual(first - 1)
        normalise_pool(first - 3, T)
        moments(first - 1)

        for i in range(first, last):
            add_residual_half(i, 1)
            if i > first:
                mean_of_halves(i - 1)
                project(i + 1, 0)
            bring_back(i + 1)
            if i > first:
                sum_squares(i - 1, 1.0, neg_mean[i - 1])
            bias_and_mask(i + 1, 0)
            add_residual_half(i, 0)
            normalise_scalar(i - 2, HALF)
            normalise_pool(i - 2, HALF)
            inverse_std(i - 1)
            if i + 1 < last:
                mean_shift(i - 1)

        add_residual_half(last, 1)
        mean_of_halves(last - 1)
        sum_squares(last - 1, 1.0, neg_mean[last - 1])
        add_residual_half(last, 0)
        normalise_vector(last - 2, 1)
        mean_of_halves(last)
        inverse_std(last - 1)
        sum_squares(last, 1.0, neg_mean[last])
        normalise_vector(last - 1, 1)
        inverse_std(last)
        normalise_vector(last, 2)
